import numpy as np
import ml_dtypes

BF16 = ml_dtypes.bfloat16


def bf(x):
    return np.asarray(x, np.float32).astype(BF16)


def f32(x):
    return np.asarray(x, np.float32)


def f64(x):
    return np.asarray(x).astype(np.float64)


def striped(idx):
    return np.tile(idx.reshape(-1, 16).T, (8, 1))


D, S, N, E, H, M = 128, 1024, 128, 4, 128, 512
EPS = 1e-5
FGATE = 0.5


def setup_inputs():
    return {
        "x": bf(np.random.standard_normal((D, S))),
        "w": bf(2.0 * np.random.standard_normal((D, M)) / np.sqrt(D)),
        "b": f32(0.1 * np.random.standard_normal((M, 1))),
        "bn_w": f32(1.0 + 0.1 * np.random.standard_normal((M, 1))),
        "bn_b": f32(0.1 * np.random.standard_normal((M, 1))),
        "run_mean": f32(0.1 * np.random.standard_normal((M, 1))),
        "run_var": f32(0.5 + 0.5 * np.abs(np.random.standard_normal((M, 1)))),
        "gate_logits": f32(np.random.standard_normal((E, N))),
        "offs": striped(np.random.permutation(S)[:N]),
    }


def reference(x, w, b, bn_w, bn_b, run_mean, run_var, gate_logits, offs):
    idx = offs[:16].T.reshape(-1)
    z = FGATE * (f64(w).T @ f64(x)[:, idx]) + f64(b)
    scale = f64(bn_w) / np.sqrt(f64(run_var) + EPS)
    shift = f64(bn_b) - f64(run_mean) * scale
    y = z * scale + shift
    a = y / (1.0 + np.exp(-y))
    p = np.exp(f64(gate_logits))
    p = p / p.sum(axis=0, keepdims=True)
    return (a.reshape(E, H, N) * p[:, None, :]).sum(axis=0)

@@ -1,0 +1,89 @@
+import concourse.mybir as mybir
+
+F32 = mybir.dt.float32
+BF16 = mybir.dt.bfloat16
+U16 = mybir.dt.uint16
+ALU = mybir.AluOpType
+FUNC = mybir.ActivationFunctionType
+AXIS = mybir.AxisListType
+
+D, S, N, E, H = 128, 1024, 128, 4, 128
+M = E * H
+EPS = 1e-5
+FGATE = 0.5
+FLOPS = 2 * D * M * N
+
+
+def tile_homelayeroptimized_kernel(
+    tc, x, w, b, bn_w, bn_b, run_mean, run_var, gate_logits, offs, out
+):
+    nc = tc.nc
+    with (
+        tc.tile_pool(name="held", bufs=1) as held,
+        tc.psum_pool(name="psum", bufs=1) as psum,
+    ):
+        offsets = held.tile([128, N // 16], U16, name="offsets")
+        nc.sync.dma_start(offsets[:], offs)
+        tokens = held.tile([D, S], BF16, name="tokens")
+        nc.sync.dma_start(tokens[:], x)
+        weights = held.tile([D, M], BF16, name="weights")
+        nc.scalar.dma_start(weights[:], w)
+
+        logits = held.tile([128, E * N], F32, name="logits")
+        nc.scalar.dma_start(logits[:], gate_logits.rearrange("e j -> (e j)").partition_broadcast(128))
+
+        per_channel = {}
+        with nc.allow_non_contiguous_dma(reason="512 single floats, one to a partition and expert"):
+            for name, vector in (("b", b), ("bn_w", bn_w), ("bn_b", bn_b), ("mean", run_mean), ("var", run_var)):
+                per_channel[name] = held.tile([H, E], F32, name=name)
+                nc.gpsimd.dma_start(per_channel[name][:], vector.rearrange("(e i) o -> i (e o)", e=E))
+
+        std = held.tile([H, E], F32, name="std")
+        nc.vector.tensor_scalar_add(std[:], per_channel["var"][:], EPS)
+        nc.scalar.activation(std[:], std[:], FUNC.Sqrt)
+        scale = held.tile([H, E], F32, name="scale")
+        nc.vector.reciprocal(scale[:], std[:])
+        nc.vector.tensor_mul(scale[:], scale[:], per_channel["bn_w"][:])
+        offset = held.tile([H, E], F32, name="offset")
+        nc.vector.tensor_sub(offset[:], per_channel["b"][:], per_channel["mean"][:])
+        nc.vector.tensor_mul(offset[:], offset[:], scale[:])
+        nc.vector.tensor_add(offset[:], offset[:], per_channel["bn_b"][:])
+        slope = held.tile([H, E], F32, name="slope")
+        nc.vector.tensor_scalar_mul(slope[:], scale[:], FGATE)
+
+        top = held.tile([128, N], F32, name="top")
+        nc.vector.tensor_reduce(top[:], logits[:].rearrange("p (e j) -> p j e", e=E), AXIS.X, ALU.max)
+        probs = held.tile([128, E * N], F32, name="probs")
+        probs_ej = probs[:].rearrange("p (e j) -> p e j", e=E)
+        nc.vector.tensor_tensor(
+            probs_ej,
+            logits[:].rearrange("p (e j) -> p e j", e=E),
+            top[:].unsqueeze(1).to_broadcast([128, E, N]),
+            ALU.subtract,
+        )
+        nc.scalar.activation(probs[:], probs[:], FUNC.Exp)
+        total = held.tile([128, N], F32, name="total")
+        nc.vector.tensor_reduce(total[:], probs[:].rearrange("p (e j) -> p j e", e=E), AXIS.X, ALU.add)
+        nc.vector.reciprocal(total[:], total[:])
+        nc.vector.tensor_tensor(probs_ej, probs_ej, total[:].unsqueeze(1).to_broadcast([128, E, N]), ALU.mult)
+
+        mixed = held.tile([H, N], F32, name="mixed")
+        for e in range(E):
+            product = psum.tile([H, N], F32, name=f"product{e}")
+            nc.tensor.matmul(
+                product[:],
+                weights[:, e * H : (e + 1) * H],
+                tokens[:].indirect(offsets[:]),
+                start=True,
+                stop=True,
+            )
+            active = held.tile([H, N], F32, name=f"active{e}")
+            nc.scalar.activation(
+                active[:], product[:], FUNC.Silu, bias=offset[:, e : e + 1], scale=slope[:, e : e + 1]
+            )
+            if e == 0:
+                nc.vector.tensor_mul(mixed[:], active[:], probs[:, 0:N])
+            else:
+                nc.vector.tensor_mul(active[:], active[:], probs[:, e * N : (e + 1) * N])
+                nc.vector.tensor_add(mixed[:], mixed[:], active[:])
+        nc.sync.dma_start(out, mixed[:])

@@ -1,4 +1,5 @@
 import concourse.mybir as mybir
+from concourse.masks import make_identity
 
 F32 = mybir.dt.float32
 BF16 = mybir.dt.bfloat16
@@ -11,7 +12,16 @@ D, S, N, E, H = 128, 1024, 128, 4, 128
 M = E * H
 EPS = 1e-5
 FGATE = 0.5
+EULER = 2.718281828459045
 FLOPS = 2 * D * M * N
+
+SMALL = ("b", "mean", "bn_w", "bn_b", "var", "gate")
+ROWS = E * len(SMALL)
+FIRST_ROW = {name: E * k for k, name in enumerate(SMALL)}
+
+
+def four(name):
+    return slice(FIRST_ROW[name], FIRST_ROW[name] + E)
 
 
 def tile_homelayeroptimized_kernel(
@@ -27,47 +37,48 @@ def tile_homelayeroptimized_kernel(
         tokens = held.tile([D, S], BF16, name="tokens")
         nc.sync.dma_start(tokens[:], x)
         weights = held.tile([D, M], BF16, name="weights")
-        nc.scalar.dma_start(weights[:], w)
+        nc.sync.dma_start(weights[:], w)
 
-        logits = held.tile([128, E * N], F32, name="logits")
-        nc.scalar.dma_start(logits[:], gate_logits.rearrange("e j -> (e j)").partition_broadcast(128))
+        rows = held.tile([ROWS, 128], F32, name="rows")
+        nc.scalar.dma_start(rows[four("gate"), :], gate_logits)
+        for name, vector in (("var", run_var), ("b", b), ("mean", run_mean), ("bn_w", bn_w), ("bn_b", bn_b)):
+            nc.scalar.dma_start(rows[four(name), :], vector.rearrange("(e i) o -> e (i o)", e=E))
 
-        per_channel = {}
-        with nc.allow_non_contiguous_dma(reason="512 single floats, one to a partition and expert"):
-            for name, vector in (("b", b), ("bn_w", bn_w), ("bn_b", bn_b), ("mean", run_mean), ("var", run_var)):
-                per_channel[name] = held.tile([H, E], F32, name=name)
-                nc.gpsimd.dma_start(per_channel[name][:], vector.rearrange("(e i) o -> i (e o)", e=E))
+        ident = held.tile([128, 128], F32, name="ident")
+        make_identity(nc, ident[:])
+        ones = held.tile([128, 128], F32, name="ones")
+        nc.vector.memset(ones[:], 1.0)
+        base = held.tile([128, 2 * E], F32, name="base")
+        exponent = held.tile([128, 2 * E], F32, name="exponent")
+        nc.vector.memset(base[:, E : 2 * E], EULER)
+        nc.vector.memset(exponent[:, 0:E], -0.5)
 
-        std = held.tile([H, E], F32, name="std")
-        nc.vector.tensor_scalar_add(std[:], per_channel["var"][:], EPS)
-        nc.scalar.activation(std[:], std[:], FUNC.Sqrt)
-        scale = held.tile([H, E], F32, name="scale")
-        nc.vector.reciprocal(scale[:], std[:])
-        nc.vector.tensor_mul(scale[:], scale[:], per_channel["bn_w"][:])
-        offset = held.tile([H, E], F32, name="offset")
-        nc.vector.tensor_sub(offset[:], per_channel["b"][:], per_channel["mean"][:])
-        nc.vector.tensor_mul(offset[:], offset[:], scale[:])
-        nc.vector.tensor_add(offset[:], offset[:], per_channel["bn_b"][:])
-        slope = held.tile([H, E], F32, name="slope")
-        nc.vector.tensor_scalar_mul(slope[:], scale[:], FGATE)
+        columns = psum.tile([128, ROWS], F32, name="columns")
+        nc.tensor.matmul(columns[:], rows[:], ident[0:ROWS, 0:ROWS], start=True, stop=True)
 
-        top = held.tile([128, N], F32, name="top")
-        nc.vector.tensor_reduce(top[:], logits[:].rearrange("p (e j) -> p j e", e=E), AXIS.X, ALU.max)
-        probs = held.tile([128, E * N], F32, name="probs")
-        probs_ej = probs[:].rearrange("p (e j) -> p e j", e=E)
-        nc.vector.tensor_tensor(
-            probs_ej,
-            logits[:].rearrange("p (e j) -> p e j", e=E),
-            top[:].unsqueeze(1).to_broadcast([128, E, N]),
-            ALU.subtract,
-        )
-        nc.scalar.activation(probs[:], probs[:], FUNC.Exp)
-        total = held.tile([128, N], F32, name="total")
-        nc.vector.tensor_reduce(total[:], probs[:].rearrange("p (e j) -> p j e", e=E), AXIS.X, ALU.add)
-        nc.vector.reciprocal(total[:], total[:])
-        nc.vector.tensor_tensor(probs_ej, probs_ej, total[:].unsqueeze(1).to_broadcast([128, E, N]), ALU.mult)
+        nc.vector.tensor_scalar_add(base[:, 0:E], columns[:, four("var")], EPS)
+        top = held.tile([128, 1], F32, name="top")
+        nc.vector.tensor_reduce(top[:], columns[:, four("gate")], AXIS.X, ALU.max)
+        nc.vector.tensor_scalar_sub(exponent[:, E : 2 * E], columns[:, four("gate")], top[:, 0:1])
+        powers = held.tile([128, 2 * E], F32, name="powers")
+        nc.gpsimd.tensor_tensor(powers[:], base[:], exponent[:], ALU.pow)
+        rstd = powers[:, 0:E]
+        expd = powers[:, E : 2 * E]
 
-        mixed = held.tile([H, N], F32, name="mixed")
+        channel = held.tile([128, 4 * E], F32, name="channel")
+        nc.vector.tensor_copy(channel[:], columns[:, 0 : 4 * E])
+        centred = held.tile([128, E], F32, name="centred")
+        nc.vector.tensor_sub(centred[:], channel[:, four("b")], channel[:, four("mean")])
+        nc.vector.tensor_mul(centred[:], centred[:], channel[:, four("bn_w")])
+        half_w = held.tile([128, E], F32, name="half_w")
+        nc.vector.tensor_scalar_mul(half_w[:], channel[:, four("bn_w")], FGATE)
+        slope = held.tile([128, E], F32, name="slope")
+        nc.gpsimd.tensor_mul(slope[:], half_w[:], rstd)
+        offset = held.tile([128, E], F32, name="offset")
+        nc.gpsimd.tensor_mul(offset[:], centred[:], rstd)
+        nc.gpsimd.tensor_add(offset[:], offset[:], channel[:, four("bn_b")])
+
+        products = []
         for e in range(E):
             product = psum.tile([H, N], F32, name=f"product{e}")
             nc.tensor.matmul(
@@ -77,13 +88,28 @@ def tile_homelayeroptimized_kernel(
                 start=True,
                 stop=True,
             )
+            products.append(product)
+
+        total = held.tile([128, 1], F32, name="total")
+        nc.vector.tensor_reduce(total[:], expd, AXIS.X, ALU.add)
+        nc.vector.reciprocal(total[:], total[:])
+        gates = psum.tile([128, E * N], F32, name="gates")
+        for e in range(E):
+            spread = held.tile([128, 128], F32, name=f"spread{e}")
+            nc.vector.tensor_scalar(
+                spread[:], ones[:], powers[:, E + e : E + e + 1], total[:, 0:1], ALU.mult, ALU.mult
+            )
+            nc.tensor.transpose(gates[:, e * N : (e + 1) * N], spread[:], ident[:])
+
+        mixed = held.tile([H, N], F32, name="mixed")
+        for e in range(E):
             active = held.tile([H, N], F32, name=f"active{e}")
             nc.scalar.activation(
-                active[:], product[:], FUNC.Silu, bias=offset[:, e : e + 1], scale=slope[:, e : e + 1]
+                active[:], products[e][:], FUNC.Silu, bias=offset[:, e : e + 1], scale=slope[:, e : e + 1]
             )
             if e == 0:
-                nc.vector.tensor_mul(mixed[:], active[:], probs[:, 0:N])
+                nc.vector.tensor_mul(mixed[:], active[:], gates[:, 0:N])
             else:
-                nc.vector.tensor_mul(active[:], active[:], probs[:, e * N : (e + 1) * N])
+                nc.vector.tensor_mul(active[:], active[:], gates[:, e * N : (e + 1) * N])
                 nc.vector.tensor_add(mixed[:], mixed[:], active[:])
         nc.sync.dma_start(out, mixed[:])

@@ -15,14 +15,6 @@ FGATE = 0.5
 EULER = 2.718281828459045
 FLOPS = 2 * D * M * N
 
-SMALL = ("b", "mean", "bn_w", "bn_b", "var", "gate")
-ROWS = E * len(SMALL)
-FIRST_ROW = {name: E * k for k, name in enumerate(SMALL)}
-
-
-def four(name):
-    return slice(FIRST_ROW[name], FIRST_ROW[name] + E)
-
 
 def tile_homelayeroptimized_kernel(
     tc, x, w, b, bn_w, bn_b, run_mean, run_var, gate_logits, offs, out
@@ -32,17 +24,24 @@ def tile_homelayeroptimized_kernel(
         tc.tile_pool(name="held", bufs=1) as held,
         tc.psum_pool(name="psum", bufs=1) as psum,
     ):
-        offsets = held.tile([128, N // 16], U16, name="offsets")
-        nc.sync.dma_start(offsets[:], offs)
+        early = held.tile([2 * E, 128], F32, name="early")
+        later = held.tile([4 * E, 128], F32, name="later")
         tokens = held.tile([D, S], BF16, name="tokens")
-        nc.sync.dma_start(tokens[:], x)
         weights = held.tile([D, M], BF16, name="weights")
-        nc.sync.dma_start(weights[:], w)
+        offsets = held.tile([128, N // 16], U16, name="offsets")
 
-        rows = held.tile([ROWS, 128], F32, name="rows")
-        nc.scalar.dma_start(rows[four("gate"), :], gate_logits)
-        for name, vector in (("var", run_var), ("b", b), ("mean", run_mean), ("bn_w", bn_w), ("bn_b", bn_b)):
-            nc.scalar.dma_start(rows[four(name), :], vector.rearrange("(e i) o -> e (i o)", e=E))
+        def as_rows(vector):
+            return vector.rearrange("(e i) o -> e (i o)", e=E)
+
+        nc.sync.dma_start(early[0:E, :], gate_logits)
+        nc.scalar.dma_start(early[E : 2 * E, :], as_rows(run_var))
+        nc.gpsimd.dma_start(later[0:E, :], as_rows(b))
+        nc.sync.dma_start(tokens[:], x)
+        nc.scalar.dma_start(weights[:], w)
+        nc.gpsimd.dma_start(later[E : 2 * E, :], as_rows(run_mean))
+        nc.sync.dma_start(offsets[:], offs)
+        nc.scalar.dma_start(later[2 * E : 3 * E, :], as_rows(bn_w))
+        nc.gpsimd.dma_start(later[3 * E : 4 * E, :], as_rows(bn_b))
 
         ident = held.tile([128, 128], F32, name="ident")
         make_identity(nc, ident[:])
@@ -52,31 +51,24 @@ def tile_homelayeroptimized_kernel(
         exponent = held.tile([128, 2 * E], F32, name="exponent")
         nc.vector.memset(base[:, E : 2 * E], EULER)
         nc.vector.memset(exponent[:, 0:E], -0.5)
+        turn = held.tile([4 * E, 3 * E], F32, name="turn")
+        nc.vector.tensor_sub(turn[:, 0:E], ident[0 : 4 * E, 0:E], ident[0 : 4 * E, E : 2 * E])
+        nc.vector.tensor_copy(turn[:, E : 3 * E], ident[0 : 4 * E, 2 * E : 4 * E])
 
-        columns = psum.tile([128, ROWS], F32, name="columns")
-        nc.tensor.matmul(columns[:], rows[:], ident[0:ROWS, 0:ROWS], start=True, stop=True)
+        gate_var = psum.tile([128, 2 * E], F32, name="gate_var")
+        nc.tensor.matmul(gate_var[:], early[:], ident[0 : 2 * E, 0 : 2 * E], start=True, stop=True)
+        channel = psum.tile([128, 3 * E], F32, name="channel")
+        nc.tensor.matmul(channel[:], later[:], turn[:], start=True, stop=True)
+        centred, gain, bias = channel[:, 0:E], channel[:, E : 2 * E], channel[:, 2 * E : 3 * E]
 
-        nc.vector.tensor_scalar_add(base[:, 0:E], columns[:, four("var")], EPS)
+        nc.vector.tensor_scalar_add(base[:, 0:E], gate_var[:, E : 2 * E], EPS)
         top = held.tile([128, 1], F32, name="top")
-        nc.vector.tensor_reduce(top[:], columns[:, four("gate")], AXIS.X, ALU.max)
-        nc.vector.tensor_scalar_sub(exponent[:, E : 2 * E], columns[:, four("gate")], top[:, 0:1])
+        nc.vector.tensor_reduce(top[:], gate_var[:, 0:E], AXIS.X, ALU.max)
+        nc.vector.tensor_scalar_sub(exponent[:, E : 2 * E], gate_var[:, 0:E], top[:, 0:1])
         powers = held.tile([128, 2 * E], F32, name="powers")
         nc.gpsimd.tensor_tensor(powers[:], base[:], exponent[:], ALU.pow)
         rstd = powers[:, 0:E]
         expd = powers[:, E : 2 * E]
-
-        channel = held.tile([128, 4 * E], F32, name="channel")
-        nc.vector.tensor_copy(channel[:], columns[:, 0 : 4 * E])
-        centred = held.tile([128, E], F32, name="centred")
-        nc.vector.tensor_sub(centred[:], channel[:, four("b")], channel[:, four("mean")])
-        nc.vector.tensor_mul(centred[:], centred[:], channel[:, four("bn_w")])
-        half_w = held.tile([128, E], F32, name="half_w")
-        nc.vector.tensor_scalar_mul(half_w[:], channel[:, four("bn_w")], FGATE)
-        slope = held.tile([128, E], F32, name="slope")
-        nc.gpsimd.tensor_mul(slope[:], half_w[:], rstd)
-        offset = held.tile([128, E], F32, name="offset")
-        nc.gpsimd.tensor_mul(offset[:], centred[:], rstd)
-        nc.gpsimd.tensor_add(offset[:], offset[:], channel[:, four("bn_b")])
 
         products = []
         for e in range(E):
@@ -90,26 +82,37 @@ def tile_homelayeroptimized_kernel(
             )
             products.append(product)
 
+        slope = held.tile([128, E], F32, name="slope")
+        nc.vector.scalar_tensor_tensor(slope[:], gain, FGATE, rstd, ALU.mult, ALU.mult)
+        offset = held.tile([128, E], F32, name="offset")
+        nc.vector.scalar_tensor_tensor(offset[:], centred, 1.0 / FGATE, slope[:], ALU.mult, ALU.mult)
+        nc.vector.tensor_add(offset[:], offset[:], bias)
+
+        active = held.tile([H, E * N], F32, name="active")
+        for e in range(E):
+            nc.scalar.activation(
+                active[:, e * N : (e + 1) * N],
+                products[e][:],
+                FUNC.Silu,
+                bias=offset[:, e : e + 1],
+                scale=slope[:, e : e + 1],
+            )
+
         total = held.tile([128, 1], F32, name="total")
         nc.vector.tensor_reduce(total[:], expd, AXIS.X, ALU.add)
         nc.vector.reciprocal(total[:], total[:])
-        gates = psum.tile([128, E * N], F32, name="gates")
+        gates = [psum.tile([128, 2 * N], F32, name=f"gates{pair}") for pair in range(E // 2)]
         for e in range(E):
             spread = held.tile([128, 128], F32, name=f"spread{e}")
             nc.vector.tensor_scalar(
                 spread[:], ones[:], powers[:, E + e : E + e + 1], total[:, 0:1], ALU.mult, ALU.mult
             )
-            nc.tensor.transpose(gates[:, e * N : (e + 1) * N], spread[:], ident[:])
+            nc.tensor.transpose(gates[e // 2][:, (e % 2) * N : (e % 2 + 1) * N], spread[:], ident[:])
 
+        for pair in range(E // 2):
+            both = active[:, pair * 2 * N : (pair + 1) * 2 * N]
+            nc.vector.tensor_mul(both, both, gates[pair][:])
+        nc.vector.tensor_add(active[:, 0 : 2 * N], active[:, 0 : 2 * N], active[:, 2 * N : 4 * N])
         mixed = held.tile([H, N], F32, name="mixed")
-        for e in range(E):
-            active = held.tile([H, N], F32, name=f"active{e}")
-            nc.scalar.activation(
-                active[:], products[e][:], FUNC.Silu, bias=offset[:, e : e + 1], scale=slope[:, e : e + 1]
-            )
-            if e == 0:
-                nc.vector.tensor_mul(mixed[:], active[:], gates[:, 0:N])
-            else:
-                nc.vector.tensor_mul(active[:], active[:], gates[:, e * N : (e + 1) * N])
-                nc.vector.tensor_add(mixed[:], mixed[:], active[:])
+        nc.vector.tensor_add(mixed[:], active[:, 0:N], active[:, N : 2 * N])
         nc.sync.dma_start(out, mixed[:])

@@ -12,7 +12,6 @@ D, S, N, E, H = 128, 1024, 128, 4, 128
 M = E * H
 EPS = 1e-5
 FGATE = 0.5
-EULER = 2.718281828459045
 FLOPS = 2 * D * M * N
 
 
@@ -35,84 +34,77 @@ def tile_homelayeroptimized_kernel(
 
         nc.sync.dma_start(early[0:E, :], gate_logits)
         nc.scalar.dma_start(early[E : 2 * E, :], as_rows(run_var))
-        nc.gpsimd.dma_start(later[0:E, :], as_rows(b))
+        nc.sync.dma_start(later[E : 2 * E, :], as_rows(run_mean))
+        nc.scalar.dma_start(later[2 * E : 3 * E, :], as_rows(bn_w))
+        nc.sync.dma_start(later[3 * E : 4 * E, :], as_rows(bn_b))
+        nc.scalar.dma_start(later[0:E, :], as_rows(b))
         nc.sync.dma_start(tokens[:], x)
         nc.scalar.dma_start(weights[:], w)
-        nc.gpsimd.dma_start(later[E : 2 * E, :], as_rows(run_mean))
         nc.sync.dma_start(offsets[:], offs)
-        nc.scalar.dma_start(later[2 * E : 3 * E, :], as_rows(bn_w))
-        nc.gpsimd.dma_start(later[3 * E : 4 * E, :], as_rows(bn_b))
 
+        small = held.tile([4 * E, 4 * E], F32, name="small")
+        make_identity(nc, small[:])
         ident = held.tile([128, 128], F32, name="ident")
-        make_identity(nc, ident[:])
+        nc.vector.memset(ident[:], 0.0)
+        make_identity(nc, ident[:], nomemset=True)
         ones = held.tile([128, 128], F32, name="ones")
         nc.vector.memset(ones[:], 1.0)
-        base = held.tile([128, 2 * E], F32, name="base")
-        exponent = held.tile([128, 2 * E], F32, name="exponent")
-        nc.vector.memset(base[:, E : 2 * E], EULER)
-        nc.vector.memset(exponent[:, 0:E], -0.5)
+        minus_half = held.tile([128, E], F32, name="minus_half")
+        nc.vector.memset(minus_half[:], -0.5)
         turn = held.tile([4 * E, 3 * E], F32, name="turn")
-        nc.vector.tensor_sub(turn[:, 0:E], ident[0 : 4 * E, 0:E], ident[0 : 4 * E, E : 2 * E])
-        nc.vector.tensor_copy(turn[:, E : 3 * E], ident[0 : 4 * E, 2 * E : 4 * E])
+        nc.vector.tensor_sub(turn[:, 0:E], small[:, 0:E], small[:, E : 2 * E])
+        nc.vector.tensor_copy(turn[:, E : 3 * E], small[:, 2 * E : 4 * E])
 
-        gate_var = psum.tile([128, 2 * E], F32, name="gate_var")
-        nc.tensor.matmul(gate_var[:], early[:], ident[0 : 2 * E, 0 : 2 * E], start=True, stop=True)
-        channel = psum.tile([128, 3 * E], F32, name="channel")
-        nc.tensor.matmul(channel[:], later[:], turn[:], start=True, stop=True)
-        centred, gain, bias = channel[:, 0:E], channel[:, E : 2 * E], channel[:, 2 * E : 3 * E]
+        bank_a = psum.tile([128, 2 * E + 3 * N], F32, name="bank_a")
+        bank_b = psum.tile([128, 3 * E + N], F32, name="bank_b")
+        gate, var = bank_a[:, 0:E], bank_a[:, E : 2 * E]
+        centred, gain, bias = bank_b[:, 0:E], bank_b[:, E : 2 * E], bank_b[:, 2 * E : 3 * E]
+        products = [bank_a[:, 2 * E + e * N : 2 * E + (e + 1) * N] for e in range(E - 1)]
+        products.append(bank_b[:, 3 * E : 3 * E + N])
+        nc.tensor.matmul(bank_a[:, 0 : 2 * E], early[:], small[0 : 2 * E, 0 : 2 * E], start=True, stop=True)
+        nc.tensor.matmul(bank_b[:, 0 : 3 * E], later[:], turn[:], start=True, stop=True)
 
-        nc.vector.tensor_scalar_add(base[:, 0:E], gate_var[:, E : 2 * E], EPS)
-        top = held.tile([128, 1], F32, name="top")
-        nc.vector.tensor_reduce(top[:], gate_var[:, 0:E], AXIS.X, ALU.max)
-        nc.vector.tensor_scalar_sub(exponent[:, E : 2 * E], gate_var[:, 0:E], top[:, 0:1])
-        powers = held.tile([128, 2 * E], F32, name="powers")
-        nc.gpsimd.tensor_tensor(powers[:], base[:], exponent[:], ALU.pow)
-        rstd = powers[:, 0:E]
-        expd = powers[:, E : 2 * E]
+        minus_top = held.tile([128, 1], F32, name="minus_top")
+        nc.vector.tensor_reduce(minus_top[:], gate, AXIS.X, ALU.max, negate=True)
+        rstd = held.tile([128, E], F32, name="rstd")
+        nc.vector.tensor_scalar_add(rstd[:], var, EPS)
+        nc.gpsimd.tensor_tensor(rstd[:], rstd[:], minus_half[:], ALU.pow)
+        expd = held.tile([128, E], F32, name="expd")
+        total = held.tile([128, 1], F32, name="total")
+        nc.scalar.activation(expd[:], gate, FUNC.Exp, bias=minus_top[:, 0:1], accum_out=total[:, 0:1])
+        nc.vector.reciprocal(total[:], total[:])
 
-        products = []
         for e in range(E):
-            product = psum.tile([H, N], F32, name=f"product{e}")
             nc.tensor.matmul(
-                product[:],
+                products[e],
                 weights[:, e * H : (e + 1) * H],
                 tokens[:].indirect(offsets[:]),
                 start=True,
                 stop=True,
             )
-            products.append(product)
 
-        slope = held.tile([128, E], F32, name="slope")
-        nc.vector.scalar_tensor_tensor(slope[:], gain, FGATE, rstd, ALU.mult, ALU.mult)
-        offset = held.tile([128, E], F32, name="offset")
-        nc.vector.scalar_tensor_tensor(offset[:], centred, 1.0 / FGATE, slope[:], ALU.mult, ALU.mult)
-        nc.vector.tensor_add(offset[:], offset[:], bias)
+        factors = held.tile([128, 2, E], F32, name="factors")
+        nc.vector.tensor_scalar_mul(factors[:, 0, :], gain, FGATE)
+        nc.vector.scalar_tensor_tensor(factors[:, 1, :], centred, 1.0 / FGATE, factors[:, 0, :], ALU.mult, ALU.mult)
+        affine = held.tile([128, 2, E], F32, name="affine")
+        nc.vector.tensor_tensor(affine[:], factors[:], rstd[:].unsqueeze(1).to_broadcast([128, 2, E]), ALU.mult)
+        nc.vector.tensor_add(affine[:, 1, :], affine[:, 1, :], bias)
 
-        active = held.tile([H, E * N], F32, name="active")
-        for e in range(E):
-            nc.scalar.activation(
-                active[:, e * N : (e + 1) * N],
-                products[e][:],
-                FUNC.Silu,
-                bias=offset[:, e : e + 1],
-                scale=slope[:, e : e + 1],
-            )
-
-        total = held.tile([128, 1], F32, name="total")
-        nc.vector.tensor_reduce(total[:], expd, AXIS.X, ALU.add)
-        nc.vector.reciprocal(total[:], total[:])
-        gates = [psum.tile([128, 2 * N], F32, name=f"gates{pair}") for pair in range(E // 2)]
+        gates = [psum.tile([128, N], F32, name=f"gates{e}") for e in range(E)]
         for e in range(E):
             spread = held.tile([128, 128], F32, name=f"spread{e}")
-            nc.vector.tensor_scalar(
-                spread[:], ones[:], powers[:, E + e : E + e + 1], total[:, 0:1], ALU.mult, ALU.mult
-            )
-            nc.tensor.transpose(gates[e // 2][:, (e % 2) * N : (e % 2 + 1) * N], spread[:], ident[:])
+            nc.vector.tensor_scalar(spread[:], ones[:], expd[:, e : e + 1], total[:, 0:1], ALU.mult, ALU.mult)
+            nc.tensor.transpose(gates[e][:], spread[:], ident[:])
 
-        for pair in range(E // 2):
-            both = active[:, pair * 2 * N : (pair + 1) * 2 * N]
-            nc.vector.tensor_mul(both, both, gates[pair][:])
-        nc.vector.tensor_add(active[:, 0 : 2 * N], active[:, 0 : 2 * N], active[:, 2 * N : 4 * N])
         mixed = held.tile([H, N], F32, name="mixed")
-        nc.vector.tensor_add(mixed[:], active[:, 0:N], active[:, N : 2 * N])
+        for e in range(E):
+            active = held.tile([H, N], F32, name=f"active{e}")
+            nc.scalar.activation(
+                active[:], products[e], FUNC.Silu, bias=affine[:, 1, e : e + 1], scale=affine[:, 0, e : e + 1]
+            )
+            if e == 0:
+                nc.vector.tensor_mul(mixed[:], active[:], gates[e][:])
+            else:
+                nc.vector.tensor_mul(active[:], active[:], gates[e][:])
+                nc.vector.tensor_add(mixed[:], mixed[:], active[:])
         nc.sync.dma_start(out, mixed[:])

@@ -55,14 +55,12 @@ def tile_homelayeroptimized_kernel(
         nc.vector.tensor_sub(turn[:, 0:E], small[:, 0:E], small[:, E : 2 * E])
         nc.vector.tensor_copy(turn[:, E : 3 * E], small[:, 2 * E : 4 * E])
 
-        bank_a = psum.tile([128, 2 * E + 3 * N], F32, name="bank_a")
-        bank_b = psum.tile([128, 3 * E + N], F32, name="bank_b")
-        gate, var = bank_a[:, 0:E], bank_a[:, E : 2 * E]
-        centred, gain, bias = bank_b[:, 0:E], bank_b[:, E : 2 * E], bank_b[:, 2 * E : 3 * E]
-        products = [bank_a[:, 2 * E + e * N : 2 * E + (e + 1) * N] for e in range(E - 1)]
-        products.append(bank_b[:, 3 * E : 3 * E + N])
-        nc.tensor.matmul(bank_a[:, 0 : 2 * E], early[:], small[0 : 2 * E, 0 : 2 * E], start=True, stop=True)
-        nc.tensor.matmul(bank_b[:, 0 : 3 * E], later[:], turn[:], start=True, stop=True)
+        gate_var = psum.tile([128, 2 * E], F32, name="gate_var")
+        nc.tensor.matmul(gate_var[:], early[:], small[0 : 2 * E, 0 : 2 * E], start=True, stop=True)
+        gate, var = gate_var[:, 0:E], gate_var[:, E : 2 * E]
+        channel = psum.tile([128, 3 * E], F32, name="channel")
+        nc.tensor.matmul(channel[:], later[:], turn[:], start=True, stop=True)
+        centred, gain, bias = channel[:, 0:E], channel[:, E : 2 * E], channel[:, 2 * E : 3 * E]
 
         minus_top = held.tile([128, 1], F32, name="minus_top")
         nc.vector.tensor_reduce(minus_top[:], gate, AXIS.X, ALU.max, negate=True)
@@ -74,9 +72,14 @@ def tile_homelayeroptimized_kernel(
         nc.scalar.activation(expd[:], gate, FUNC.Exp, bias=minus_top[:, 0:1], accum_out=total[:, 0:1])
         nc.vector.reciprocal(total[:], total[:])
 
+        banks = [psum.tile([128, 4 * N], F32, name=f"bank{pair}") for pair in range(E // 2)]
+        for e in range(E):
+            spread = held.tile([128, 128], F32, name=f"spread{e}")
+            nc.vector.tensor_scalar(spread[:], ones[:], expd[:, e : e + 1], total[:, 0:1], ALU.mult, ALU.mult)
+            nc.tensor.transpose(banks[e // 2][:, (e % 2) * N : (e % 2 + 1) * N], spread[:], ident[:])
         for e in range(E):
             nc.tensor.matmul(
-                products[e],
+                banks[e // 2][:, (2 + e % 2) * N : (3 + e % 2) * N],
                 weights[:, e * H : (e + 1) * H],
                 tokens[:].indirect(offsets[:]),
                 start=True,
@@ -90,21 +93,19 @@ def tile_homelayeroptimized_kernel(
         nc.vector.tensor_tensor(affine[:], factors[:], rstd[:].unsqueeze(1).to_broadcast([128, 2, E]), ALU.mult)
         nc.vector.tensor_add(affine[:, 1, :], affine[:, 1, :], bias)
 
-        gates = [psum.tile([128, N], F32, name=f"gates{e}") for e in range(E)]
+        active = held.tile([H, E * N], F32, name="active")
         for e in range(E):
-            spread = held.tile([128, 128], F32, name=f"spread{e}")
-            nc.vector.tensor_scalar(spread[:], ones[:], expd[:, e : e + 1], total[:, 0:1], ALU.mult, ALU.mult)
-            nc.tensor.transpose(gates[e][:], spread[:], ident[:])
-
-        mixed = held.tile([H, N], F32, name="mixed")
-        for e in range(E):
-            active = held.tile([H, N], F32, name=f"active{e}")
             nc.scalar.activation(
-                active[:], products[e], FUNC.Silu, bias=affine[:, 1, e : e + 1], scale=affine[:, 0, e : e + 1]
+                active[:, e * N : (e + 1) * N],
+                banks[e // 2][:, (2 + e % 2) * N : (3 + e % 2) * N],
+                FUNC.Silu,
+                bias=affine[:, 1, e : e + 1],
+                scale=affine[:, 0, e : e + 1],
             )
-            if e == 0:
-                nc.vector.tensor_mul(mixed[:], active[:], gates[e][:])
-            else:
-                nc.vector.tensor_mul(active[:], active[:], gates[e][:])
-                nc.vector.tensor_add(mixed[:], mixed[:], active[:])
+        for pair in range(E // 2):
+            both = active[:, pair * 2 * N : (pair + 1) * 2 * N]
+            nc.vector.tensor_mul(both, both, banks[pair][:, 0 : 2 * N])
+        nc.vector.tensor_add(active[:, 0 : 2 * N], active[:, 0 : 2 * N], active[:, 2 * N : 4 * N])
+        mixed = held.tile([H, N], F32, name="mixed")
+        nc.vector.tensor_add(mixed[:], active[:, 0:N], active[:, N : 2 * N])
         nc.sync.dma_start(out, mixed[:])

@@ -55,12 +55,14 @@ def tile_homelayeroptimized_kernel(
         nc.vector.tensor_sub(turn[:, 0:E], small[:, 0:E], small[:, E : 2 * E])
         nc.vector.tensor_copy(turn[:, E : 3 * E], small[:, 2 * E : 4 * E])
 
-        gate_var = psum.tile([128, 2 * E], F32, name="gate_var")
-        nc.tensor.matmul(gate_var[:], early[:], small[0 : 2 * E, 0 : 2 * E], start=True, stop=True)
-        gate, var = gate_var[:, 0:E], gate_var[:, E : 2 * E]
-        channel = psum.tile([128, 3 * E], F32, name="channel")
-        nc.tensor.matmul(channel[:], later[:], turn[:], start=True, stop=True)
-        centred, gain, bias = channel[:, 0:E], channel[:, E : 2 * E], channel[:, 2 * E : 3 * E]
+        bank_a = psum.tile([128, 2 * E + 3 * N], F32, name="bank_a")
+        bank_b = psum.tile([128, 3 * E + N], F32, name="bank_b")
+        gate, var = bank_a[:, 0:E], bank_a[:, E : 2 * E]
+        centred, gain, bias = bank_b[:, 0:E], bank_b[:, E : 2 * E], bank_b[:, 2 * E : 3 * E]
+        products = [bank_a[:, 2 * E + e * N : 2 * E + (e + 1) * N] for e in range(E - 1)]
+        products.append(bank_b[:, 3 * E : 3 * E + N])
+        nc.tensor.matmul(bank_a[:, 0 : 2 * E], early[:], small[0 : 2 * E, 0 : 2 * E], start=True, stop=True)
+        nc.tensor.matmul(bank_b[:, 0 : 3 * E], later[:], turn[:], start=True, stop=True)
 
         minus_top = held.tile([128, 1], F32, name="minus_top")
         nc.vector.tensor_reduce(minus_top[:], gate, AXIS.X, ALU.max, negate=True)
@@ -72,14 +74,9 @@ def tile_homelayeroptimized_kernel(
         nc.scalar.activation(expd[:], gate, FUNC.Exp, bias=minus_top[:, 0:1], accum_out=total[:, 0:1])
         nc.vector.reciprocal(total[:], total[:])
 
-        banks = [psum.tile([128, 4 * N], F32, name=f"bank{pair}") for pair in range(E // 2)]
-        for e in range(E):
-            spread = held.tile([128, 128], F32, name=f"spread{e}")
-            nc.vector.tensor_scalar(spread[:], ones[:], expd[:, e : e + 1], total[:, 0:1], ALU.mult, ALU.mult)
-            nc.tensor.transpose(banks[e // 2][:, (e % 2) * N : (e % 2 + 1) * N], spread[:], ident[:])
         for e in range(E):
             nc.tensor.matmul(
-                banks[e // 2][:, (2 + e % 2) * N : (3 + e % 2) * N],
+                products[e],
                 weights[:, e * H : (e + 1) * H],
                 tokens[:].indirect(offsets[:]),
                 start=True,
@@ -93,18 +90,25 @@ def tile_homelayeroptimized_kernel(
         nc.vector.tensor_tensor(affine[:], factors[:], rstd[:].unsqueeze(1).to_broadcast([128, 2, E]), ALU.mult)
         nc.vector.tensor_add(affine[:, 1, :], affine[:, 1, :], bias)
 
+        gates = [psum.tile([128, 2 * N], F32, name=f"gates{pair}") for pair in range(E // 2)]
+        for e in range(E):
+            spread = held.tile([128, 128], F32, name=f"spread{e}")
+            nc.vector.tensor_scalar(spread[:], ones[:], expd[:, e : e + 1], total[:, 0:1], ALU.mult, ALU.mult)
+            nc.tensor.transpose(gates[e // 2][:, (e % 2) * N : (e % 2 + 1) * N], spread[:], ident[:])
+
         active = held.tile([H, E * N], F32, name="active")
         for e in range(E):
             nc.scalar.activation(
                 active[:, e * N : (e + 1) * N],
-                banks[e // 2][:, (2 + e % 2) * N : (3 + e % 2) * N],
+                products[e],
                 FUNC.Silu,
                 bias=affine[:, 1, e : e + 1],
                 scale=affine[:, 0, e : e + 1],
             )
+
         for pair in range(E // 2):
             both = active[:, pair * 2 * N : (pair + 1) * 2 * N]
-            nc.vector.tensor_mul(both, both, banks[pair][:, 0 : 2 * N])
+            nc.vector.tensor_mul(both, both, gates[pair][:])
         nc.vector.tensor_add(active[:, 0 : 2 * N], active[:, 0 : 2 * N], active[:, 2 * N : 4 * N])
         mixed = held.tile([H, N], F32, name="mixed")
         nc.vector.tensor_add(mixed[:], active[:, 0:N], active[:, N : 2 * N])

@@ -51,6 +51,11 @@ def tile_homelayeroptimized_kernel(
         nc.vector.memset(ones[:], 1.0)
         minus_half = held.tile([128, E], F32, name="minus_half")
         nc.vector.memset(minus_half[:], -0.5)
+        halve = held.tile([2 * E, 2 * E], F32, name="halve")
+        nc.vector.tensor_scalar_mul(halve[:, 0:E], small[0 : 2 * E, 0:E], 0.5)
+        nc.vector.tensor_copy(halve[:, E : 2 * E], small[0 : 2 * E, E : 2 * E])
+        warm = held.tile([128, E], F32, name="warm")
+        nc.scalar.activation(warm[:], minus_half[:], FUNC.Silu)
         turn = held.tile([4 * E, 3 * E], F32, name="turn")
         nc.vector.tensor_sub(turn[:, 0:E], small[:, 0:E], small[:, E : 2 * E])
         nc.vector.tensor_copy(turn[:, E : 3 * E], small[:, 2 * E : 4 * E])
@@ -61,17 +66,28 @@ def tile_homelayeroptimized_kernel(
         centred, gain, bias = bank_b[:, 0:E], bank_b[:, E : 2 * E], bank_b[:, 2 * E : 3 * E]
         products = [bank_a[:, 2 * E + e * N : 2 * E + (e + 1) * N] for e in range(E - 1)]
         products.append(bank_b[:, 3 * E : 3 * E + N])
-        nc.tensor.matmul(bank_a[:, 0 : 2 * E], early[:], small[0 : 2 * E, 0 : 2 * E], start=True, stop=True)
+        nc.tensor.matmul(bank_a[:, 0 : 2 * E], early[:], halve[:], start=True, stop=True)
         nc.tensor.matmul(bank_b[:, 0 : 3 * E], later[:], turn[:], start=True, stop=True)
+
+        factors = held.tile([128, 2, E], F32, name="factors")
+        nc.vector.tensor_scalar_mul(factors[:, 0, :], gain, FGATE)
+        nc.vector.scalar_tensor_tensor(factors[:, 1, :], centred, 1.0 / FGATE, factors[:, 0, :], ALU.mult, ALU.mult)
+        shift = held.tile([128, E], F32, name="shift")
+        nc.vector.tensor_copy(shift[:], bias)
 
         minus_top = held.tile([128, 1], F32, name="minus_top")
         nc.vector.tensor_reduce(minus_top[:], gate, AXIS.X, ALU.max, negate=True)
         rstd = held.tile([128, E], F32, name="rstd")
         nc.vector.tensor_scalar_add(rstd[:], var, EPS)
         nc.gpsimd.tensor_tensor(rstd[:], rstd[:], minus_half[:], ALU.pow)
+        tanh = held.tile([128, E], F32, name="tanh")
+        nc.scalar.activation(tanh[:], gate, FUNC.Tanh, bias=minus_top[:, 0:1])
+        below = held.tile([128, E], F32, name="below")
+        nc.vector.tensor_scalar(below[:], tanh[:], -1.0, 1.0, ALU.mult, ALU.add)
+        nc.vector.reciprocal(below[:], below[:])
         expd = held.tile([128, E], F32, name="expd")
         total = held.tile([128, 1], F32, name="total")
-        nc.scalar.activation(expd[:], gate, FUNC.Exp, bias=minus_top[:, 0:1], accum_out=total[:, 0:1])
+        nc.vector.scalar_tensor_tensor(expd[:], tanh[:], 1.0, below[:], ALU.add, ALU.mult, accum_out=total[:, 0:1])
         nc.vector.reciprocal(total[:], total[:])
 
         for e in range(E):
@@ -83,33 +99,32 @@ def tile_homelayeroptimized_kernel(
                 stop=True,
             )
 
-        factors = held.tile([128, 2, E], F32, name="factors")
-        nc.vector.tensor_scalar_mul(factors[:, 0, :], gain, FGATE)
-        nc.vector.scalar_tensor_tensor(factors[:, 1, :], centred, 1.0 / FGATE, factors[:, 0, :], ALU.mult, ALU.mult)
         affine = held.tile([128, 2, E], F32, name="affine")
         nc.vector.tensor_tensor(affine[:], factors[:], rstd[:].unsqueeze(1).to_broadcast([128, 2, E]), ALU.mult)
-        nc.vector.tensor_add(affine[:, 1, :], affine[:, 1, :], bias)
+        nc.vector.tensor_add(affine[:, 1, :], affine[:, 1, :], shift[:])
 
-        gates = [psum.tile([128, 2 * N], F32, name=f"gates{pair}") for pair in range(E // 2)]
+        gates = [psum.tile([128, N], F32, name=f"gates{e}") for e in range(E)]
         for e in range(E):
             spread = held.tile([128, 128], F32, name=f"spread{e}")
             nc.vector.tensor_scalar(spread[:], ones[:], expd[:, e : e + 1], total[:, 0:1], ALU.mult, ALU.mult)
-            nc.tensor.transpose(gates[e // 2][:, (e % 2) * N : (e % 2 + 1) * N], spread[:], ident[:])
+            nc.tensor.transpose(gates[e][:], spread[:], ident[:])
 
-        active = held.tile([H, E * N], F32, name="active")
+        mixed = None
         for e in range(E):
+            active = held.tile([H, N], F32, name=f"active{e}")
             nc.scalar.activation(
-                active[:, e * N : (e + 1) * N],
+                active[:],
                 products[e],
                 FUNC.Silu,
                 bias=affine[:, 1, e : e + 1],
                 scale=affine[:, 0, e : e + 1],
             )
-
-        for pair in range(E // 2):
-            both = active[:, pair * 2 * N : (pair + 1) * 2 * N]
-            nc.vector.tensor_mul(both, both, gates[pair][:])
-        nc.vector.tensor_add(active[:, 0 : 2 * N], active[:, 0 : 2 * N], active[:, 2 * N : 4 * N])
-        mixed = held.tile([H, N], F32, name="mixed")
-        nc.vector.tensor_add(mixed[:], active[:, 0:N], active[:, N : 2 * N])
+            weighed = held.tile([H, N], F32, name=f"weighed{e}")
+            nc.vector.tensor_mul(weighed[:], active[:], gates[e][:])
+            if mixed is None:
+                mixed = weighed
+            else:
+                summed = held.tile([H, N], F32, name=f"summed{e}")
+                nc.vector.tensor_add(summed[:], mixed[:], weighed[:])
+                mixed = summed
         nc.sync.dma_start(out, mixed[:])

@@ -100,8 +100,8 @@ def tile_homelayeroptimized_kernel(
             )
 
         affine = held.tile([128, 2, E], F32, name="affine")
-        nc.vector.tensor_tensor(affine[:], factors[:], rstd[:].unsqueeze(1).to_broadcast([128, 2, E]), ALU.mult)
-        nc.vector.tensor_add(affine[:, 1, :], affine[:, 1, :], shift[:])
+        nc.gpsimd.tensor_tensor(affine[:], factors[:], rstd[:].unsqueeze(1).to_broadcast([128, 2, E]), ALU.mult)
+        nc.gpsimd.tensor_tensor(affine[:, 1, :], affine[:, 1, :], shift[:], ALU.add)
 
         gates = [psum.tile([128, N], F32, name=f"gates{e}") for e in range(E)]
         for e in range(E):

@@ -42,11 +42,10 @@ def tile_homelayeroptimized_kernel(
         nc.scalar.dma_start(weights[:], w)
         nc.sync.dma_start(offsets[:], offs)
 
-        small = held.tile([4 * E, 4 * E], F32, name="small")
-        make_identity(nc, small[:])
         ident = held.tile([128, 128], F32, name="ident")
         nc.vector.memset(ident[:], 0.0)
         make_identity(nc, ident[:], nomemset=True)
+        small = ident[0 : 4 * E, 0 : 4 * E]
         ones = held.tile([128, 128], F32, name="ones")
         nc.vector.memset(ones[:], 1.0)
         minus_half = held.tile([128, E], F32, name="minus_half")

@@ -24,7 +24,8 @@ def tile_homelayeroptimized_kernel(
         tc.psum_pool(name="psum", bufs=1) as psum,
     ):
         early = held.tile([2 * E, 128], F32, name="early")
-        later = held.tile([4 * E, 128], F32, name="later")
+        later = held.tile([3 * E, 128], F32, name="later")
+        shift = held.tile([H, E], F32, name="shift")
         tokens = held.tile([D, S], BF16, name="tokens")
         weights = held.tile([D, M], BF16, name="weights")
         offsets = held.tile([128, N // 16], U16, name="offsets")
@@ -36,16 +37,16 @@ def tile_homelayeroptimized_kernel(
         nc.scalar.dma_start(early[E : 2 * E, :], as_rows(run_var))
         nc.sync.dma_start(later[E : 2 * E, :], as_rows(run_mean))
         nc.scalar.dma_start(later[2 * E : 3 * E, :], as_rows(bn_w))
-        nc.sync.dma_start(later[3 * E : 4 * E, :], as_rows(bn_b))
         nc.scalar.dma_start(later[0:E, :], as_rows(b))
         nc.sync.dma_start(tokens[:], x)
         nc.scalar.dma_start(weights[:], w)
         nc.sync.dma_start(offsets[:], offs)
+        nc.sync.dma_start(shift[:], bn_b.rearrange("(e i) o -> i (e o)", e=E))
 
         ident = held.tile([128, 128], F32, name="ident")
         nc.vector.memset(ident[:], 0.0)
         make_identity(nc, ident[:], nomemset=True)
-        small = ident[0 : 4 * E, 0 : 4 * E]
+        small = ident[0 : 3 * E, 0 : 3 * E]
         ones = held.tile([128, 128], F32, name="ones")
         nc.vector.memset(ones[:], 1.0)
         minus_half = held.tile([128, E], F32, name="minus_half")
@@ -55,24 +56,22 @@ def tile_homelayeroptimized_kernel(
         nc.vector.tensor_copy(halve[:, E : 2 * E], small[0 : 2 * E, E : 2 * E])
         warm = held.tile([128, E], F32, name="warm")
         nc.scalar.activation(warm[:], minus_half[:], FUNC.Silu)
-        turn = held.tile([4 * E, 3 * E], F32, name="turn")
+        turn = held.tile([3 * E, 2 * E], F32, name="turn")
         nc.vector.tensor_sub(turn[:, 0:E], small[:, 0:E], small[:, E : 2 * E])
-        nc.vector.tensor_copy(turn[:, E : 3 * E], small[:, 2 * E : 4 * E])
+        nc.vector.tensor_copy(turn[:, E : 2 * E], small[:, 2 * E : 3 * E])
 
         bank_a = psum.tile([128, 2 * E + 3 * N], F32, name="bank_a")
-        bank_b = psum.tile([128, 3 * E + N], F32, name="bank_b")
+        bank_b = psum.tile([128, 2 * E + N], F32, name="bank_b")
         gate, var = bank_a[:, 0:E], bank_a[:, E : 2 * E]
-        centred, gain, bias = bank_b[:, 0:E], bank_b[:, E : 2 * E], bank_b[:, 2 * E : 3 * E]
+        centred, gain = bank_b[:, 0:E], bank_b[:, E : 2 * E]
         products = [bank_a[:, 2 * E + e * N : 2 * E + (e + 1) * N] for e in range(E - 1)]
-        products.append(bank_b[:, 3 * E : 3 * E + N])
+        products.append(bank_b[:, 2 * E : 2 * E + N])
         nc.tensor.matmul(bank_a[:, 0 : 2 * E], early[:], halve[:], start=True, stop=True)
-        nc.tensor.matmul(bank_b[:, 0 : 3 * E], later[:], turn[:], start=True, stop=True)
+        nc.tensor.matmul(bank_b[:, 0 : 2 * E], later[:], turn[:], start=True, stop=True)
 
         factors = held.tile([128, 2, E], F32, name="factors")
         nc.vector.tensor_scalar_mul(factors[:, 0, :], gain, FGATE)
         nc.vector.scalar_tensor_tensor(factors[:, 1, :], centred, 1.0 / FGATE, factors[:, 0, :], ALU.mult, ALU.mult)
-        shift = held.tile([128, E], F32, name="shift")
-        nc.vector.tensor_copy(shift[:], bias)
 
         minus_top = held.tile([128, 1], F32, name="minus_top")
         nc.vector.tensor_reduce(minus_top[:], gate, AXIS.X, ALU.max, negate=True)

@@ -121,8 +121,13 @@ def tile_homelayeroptimized_kernel(
             nc.vector.tensor_mul(weighed[:], active[:], gates[e][:])
             if mixed is None:
                 mixed = weighed
-            else:
+            elif e < E - 1:
                 summed = held.tile([H, N], F32, name=f"summed{e}")
                 nc.vector.tensor_add(summed[:], mixed[:], weighed[:])
                 mixed = summed
-        nc.sync.dma_start(out, mixed[:])
+            else:
+                summed = held.tile([H, N], F32, name=f"summed{e}")
+                for queue, first in ((nc.sync, 0), (nc.scalar, N // 2)):
+                    half = slice(first, first + N // 2)
+                    nc.vector.tensor_add(summed[:, half], mixed[:, half], weighed[:, half])
+                    queue.dma_start(out[:, half], summed[:, half])

@@ -47,46 +47,56 @@ def tile_homelayeroptimized_kernel(
         nc.vector.memset(ident[:], 0.0)
         make_identity(nc, ident[:], nomemset=True)
         small = ident[0 : 3 * E, 0 : 3 * E]
-        ones = held.tile([128, 128], F32, name="ones")
-        nc.vector.memset(ones[:], 1.0)
         minus_half = held.tile([128, E], F32, name="minus_half")
         nc.vector.memset(minus_half[:], -0.5)
-        halve = held.tile([2 * E, 2 * E], F32, name="halve")
-        nc.vector.tensor_scalar_mul(halve[:, 0:E], small[0 : 2 * E, 0:E], 0.5)
-        nc.vector.tensor_copy(halve[:, E : 2 * E], small[0 : 2 * E, E : 2 * E])
+        differ = held.tile([2 * E, E * E + E], F32, name="differ")
+        unit = small[0 : 2 * E, 0:E]
+        nc.vector.tensor_sub(
+            differ[:, 0 : E * E].rearrange("k (e t) -> k e t", e=E),
+            unit.unsqueeze(2).to_broadcast([2 * E, E, E]),
+            unit.unsqueeze(1).to_broadcast([2 * E, E, E]),
+        )
+        nc.vector.tensor_copy(differ[:, E * E : E * E + E], small[0 : 2 * E, E : 2 * E])
+        terms = held.tile([128, E, E + 1], F32, name="terms")
+        nc.vector.memset(terms[:], -0.5 * E)
         warm = held.tile([128, E], F32, name="warm")
         nc.scalar.activation(warm[:], minus_half[:], FUNC.Silu)
         turn = held.tile([3 * E, 2 * E], F32, name="turn")
-        nc.vector.tensor_sub(turn[:, 0:E], small[:, 0:E], small[:, E : 2 * E])
-        nc.vector.tensor_copy(turn[:, E : 2 * E], small[:, 2 * E : 3 * E])
+        nc.vector.tensor_scalar_mul(turn[:, 0:E], small[:, 2 * E : 3 * E], FGATE)
+        nc.vector.tensor_sub(turn[:, E : 2 * E], small[:, 0:E], small[:, E : 2 * E])
+        nc.vector.tensor_scalar_mul(turn[:, E : 2 * E], turn[:, E : 2 * E], 1.0 / FGATE)
 
-        bank_a = psum.tile([128, 2 * E + 3 * N], F32, name="bank_a")
-        bank_b = psum.tile([128, 2 * E + N], F32, name="bank_b")
-        gate, var = bank_a[:, 0:E], bank_a[:, E : 2 * E]
-        centred, gain = bank_b[:, 0:E], bank_b[:, E : 2 * E]
-        products = [bank_a[:, 2 * E + e * N : 2 * E + (e + 1) * N] for e in range(E - 1)]
-        products.append(bank_b[:, 2 * E : 2 * E + N])
-        nc.tensor.matmul(bank_a[:, 0 : 2 * E], early[:], halve[:], start=True, stop=True)
-        nc.tensor.matmul(bank_b[:, 0 : 2 * E], later[:], turn[:], start=True, stop=True)
+        columns_a = E * E + E
+        columns_b = 2 * E
+        bank_a = psum.tile([128, columns_a + 2 * N], F32, name="bank_a")
+        bank_b = psum.tile([128, columns_b + 2 * N], F32, name="bank_b")
+        differences, var = bank_a[:, 0 : E * E], bank_a[:, E * E : columns_a]
+        products = []
+        for first in (0, N):
+            products.append(bank_a[:, columns_a + first : columns_a + first + N])
+            products.append(bank_b[:, columns_b + first : columns_b + first + N])
+        nc.tensor.matmul(bank_a[:, 0:columns_a], early[:], differ[:], start=True, stop=True)
+        nc.tensor.matmul(bank_b[:, 0:columns_b], later[:], turn[:], start=True, stop=True)
 
         factors = held.tile([128, 2, E], F32, name="factors")
-        nc.vector.tensor_scalar_mul(factors[:, 0, :], gain, FGATE)
-        nc.vector.scalar_tensor_tensor(factors[:, 1, :], centred, 1.0 / FGATE, factors[:, 0, :], ALU.mult, ALU.mult)
+        nc.scalar.copy(factors[:], bank_b[:, 0:columns_b].rearrange("p (v e) -> p v e", v=2))
+        nc.vector.tensor_tensor(factors[:, 1, :], factors[:, 1, :], factors[:, 0, :], ALU.mult)
 
-        minus_top = held.tile([128, 1], F32, name="minus_top")
-        nc.vector.tensor_reduce(minus_top[:], gate, AXIS.X, ALU.max, negate=True)
         rstd = held.tile([128, E], F32, name="rstd")
-        nc.vector.tensor_scalar_add(rstd[:], var, EPS)
+        nc.scalar.activation(rstd[:], var, FUNC.Copy, bias=EPS)
         nc.gpsimd.tensor_tensor(rstd[:], rstd[:], minus_half[:], ALU.pow)
-        tanh = held.tile([128, E], F32, name="tanh")
-        nc.scalar.activation(tanh[:], gate, FUNC.Tanh, bias=minus_top[:, 0:1])
-        below = held.tile([128, E], F32, name="below")
-        nc.vector.tensor_scalar(below[:], tanh[:], -1.0, 1.0, ALU.mult, ALU.add)
-        nc.vector.reciprocal(below[:], below[:])
-        expd = held.tile([128, E], F32, name="expd")
-        total = held.tile([128, 1], F32, name="total")
-        nc.vector.scalar_tensor_tensor(expd[:], tanh[:], 1.0, below[:], ALU.add, ALU.mult, accum_out=total[:, 0:1])
-        nc.vector.reciprocal(total[:], total[:])
+
+        tanh = held.tile([128, E * E], F32, name="tanh")
+        nc.scalar.activation(tanh[:], differences, FUNC.Tanh, scale=0.5)
+        raised = held.tile([128, E, E], F32, name="raised")
+        nc.vector.tensor_scalar(
+            raised[:], tanh[:].rearrange("p (e t) -> p e t", e=E), 1.0, 2.0**-24, ALU.add, ALU.max
+        )
+        nc.vector.reciprocal(terms[:, :, 0:E], raised[:])
+        total = held.tile([128, E], F32, name="total")
+        nc.vector.tensor_reduce(total[:], terms[:], AXIS.X, ALU.add)
+        twice_prob = held.tile([128, E], F32, name="twice_prob")
+        nc.vector.reciprocal(twice_prob[:], total[:])
 
         for e in range(E):
             nc.tensor.matmul(
@@ -103,9 +113,8 @@ def tile_homelayeroptimized_kernel(
 
         gates = [psum.tile([128, N], F32, name=f"gates{e}") for e in range(E)]
         for e in range(E):
-            spread = held.tile([128, 128], F32, name=f"spread{e}")
-            nc.vector.tensor_scalar(spread[:], ones[:], expd[:, e : e + 1], total[:, 0:1], ALU.mult, ALU.mult)
-            nc.tensor.transpose(gates[e][:], spread[:], ident[:])
+            spread = twice_prob[:, e : e + 1].to_broadcast([128, 128])
+            nc.tensor.transpose(gates[e][:], spread, ident[:])
 
         mixed = None
         for e in range(E):
@@ -118,7 +127,7 @@ def tile_homelayeroptimized_kernel(
                 scale=affine[:, 0, e : e + 1],
             )
             weighed = held.tile([H, N], F32, name=f"weighed{e}")
-            nc.vector.tensor_mul(weighed[:], active[:], gates[e][:])
+            nc.vector.scalar_tensor_tensor(weighed[:], active[:], 0.5, gates[e][:], ALU.mult, ALU.mult)
             if mixed is None:
                 mixed = weighed
             elif e < E - 1:

@@ -25,7 +25,7 @@ def tile_homelayeroptimized_kernel(
     ):
         early = held.tile([2 * E, 128], F32, name="early")
         later = held.tile([3 * E, 128], F32, name="later")
-        shift = held.tile([H, E], F32, name="shift")
+        base = held.tile([H, 2, E], F32, name="base")
         tokens = held.tile([D, S], BF16, name="tokens")
         weights = held.tile([D, M], BF16, name="weights")
         offsets = held.tile([128, N // 16], U16, name="offsets")
@@ -41,7 +41,8 @@ def tile_homelayeroptimized_kernel(
         nc.sync.dma_start(tokens[:], x)
         nc.scalar.dma_start(weights[:], w)
         nc.sync.dma_start(offsets[:], offs)
-        nc.sync.dma_start(shift[:], bn_b.rearrange("(e i) o -> i (e o)", e=E))
+        nc.sync.dma_start(base[:, 1, :], bn_b.rearrange("(e i) o -> i (e o)", e=E))
+        nc.vector.memset(base[:, 0, :], 0.0)
 
         ident = held.tile([128, 128], F32, name="ident")
         nc.vector.memset(ident[:], 0.0)
@@ -57,7 +58,7 @@ def tile_homelayeroptimized_kernel(
             unit.unsqueeze(1).to_broadcast([2 * E, E, E]),
         )
         nc.vector.tensor_copy(differ[:, E * E : E * E + E], small[0 : 2 * E, E : 2 * E])
-        terms = held.tile([128, E, E + 1], F32, name="terms")
+        terms = held.tile([128, E, E + 1], F32, name="terms", tag="terms")
         nc.vector.memset(terms[:], -0.5 * E)
         warm = held.tile([128, E], F32, name="warm")
         nc.scalar.activation(warm[:], minus_half[:], FUNC.Silu)
@@ -79,8 +80,11 @@ def tile_homelayeroptimized_kernel(
         nc.tensor.matmul(bank_b[:, 0:columns_b], later[:], turn[:], start=True, stop=True)
 
         factors = held.tile([128, 2, E], F32, name="factors")
-        nc.scalar.copy(factors[:], bank_b[:, 0:columns_b].rearrange("p (v e) -> p v e", v=2))
-        nc.vector.tensor_tensor(factors[:, 1, :], factors[:, 1, :], factors[:, 0, :], ALU.mult)
+        nc.scalar.copy(factors[:, 0, :], bank_b[:, 0:E])
+        for e in range(E):
+            nc.scalar.activation(
+                factors[:, 1, e : e + 1], bank_b[:, E + e : E + e + 1], FUNC.Copy, scale=factors[:, 0, e : e + 1]
+            )
 
         rstd = held.tile([128, E], F32, name="rstd")
         nc.scalar.activation(rstd[:], var, FUNC.Copy, bias=EPS)
@@ -107,36 +111,37 @@ def tile_homelayeroptimized_kernel(
                 stop=True,
             )
 
-        affine = held.tile([128, 2, E], F32, name="affine")
-        nc.gpsimd.tensor_tensor(affine[:], factors[:], rstd[:].unsqueeze(1).to_broadcast([128, 2, E]), ALU.mult)
-        nc.gpsimd.tensor_tensor(affine[:, 1, :], affine[:, 1, :], shift[:], ALU.add)
+        affine = held.tile([128, 2, E], F32, name="affine", tag="terms")
+        for e in range(E):
+            nc.vector.scalar_tensor_tensor(
+                affine[:, :, e], factors[:, :, e], rstd[:, e : e + 1], base[:, :, e], ALU.mult, ALU.add
+            )
 
         gates = [psum.tile([128, N], F32, name=f"gates{e}") for e in range(E)]
         for e in range(E):
             spread = twice_prob[:, e : e + 1].to_broadcast([128, 128])
             nc.tensor.transpose(gates[e][:], spread, ident[:])
 
-        mixed = None
-        for e in range(E):
-            active = held.tile([H, N], F32, name=f"active{e}")
-            nc.scalar.activation(
-                active[:],
-                products[e],
-                FUNC.Silu,
-                bias=affine[:, 1, e : e + 1],
-                scale=affine[:, 0, e : e + 1],
-            )
-            weighed = held.tile([H, N], F32, name=f"weighed{e}")
-            nc.vector.scalar_tensor_tensor(weighed[:], active[:], 0.5, gates[e][:], ALU.mult, ALU.mult)
-            if mixed is None:
-                mixed = weighed
-            elif e < E - 1:
-                summed = held.tile([H, N], F32, name=f"summed{e}")
-                nc.vector.tensor_add(summed[:], mixed[:], weighed[:])
-                mixed = summed
-            else:
-                summed = held.tile([H, N], F32, name=f"summed{e}")
-                for queue, first in ((nc.sync, 0), (nc.scalar, N // 2)):
-                    half = slice(first, first + N // 2)
-                    nc.vector.tensor_add(summed[:, half], mixed[:, half], weighed[:, half])
-                    queue.dma_start(out[:, half], summed[:, half])
+        sums = []
+        for pair in range(E // 2):
+            weighed = []
+            for e in (2 * pair, 2 * pair + 1):
+                active = held.tile([H, N], F32, name=f"active{e}")
+                nc.scalar.activation(
+                    active[:],
+                    products[e],
+                    FUNC.Silu,
+                    bias=affine[:, 1, e : e + 1],
+                    scale=affine[:, 0, e : e + 1],
+                )
+                share = held.tile([H, N], F32, name=f"share{e}")
+                nc.vector.scalar_tensor_tensor(share[:], active[:], 0.5, gates[e][:], ALU.mult, ALU.mult)
+                weighed.append(share)
+            both = held.tile([H, N], F32, name=f"both{pair}")
+            nc.vector.tensor_add(both[:], weighed[0][:], weighed[1][:])
+            sums.append(both)
+        summed = held.tile([H, N], F32, name="summed")
+        for queue, first in ((nc.sync, 0), (nc.scalar, N // 2)):
+            half = slice(first, first + N // 2)
+            nc.vector.tensor_add(summed[:, half], sums[0][:, half], sums[1][:, half])
+            queue.dma_start(out[:, half], summed[:, half])

@@ -80,10 +80,10 @@ def tile_homelayeroptimized_kernel(
         nc.tensor.matmul(bank_b[:, 0:columns_b], later[:], turn[:], start=True, stop=True)
 
         factors = held.tile([128, 2, E], F32, name="factors")
-        nc.scalar.copy(factors[:, 0, :], bank_b[:, 0:E])
+        nc.scalar.copy(factors[:], bank_b[:, 0:columns_b].rearrange("p (v e) -> p v e", v=2))
         for e in range(E):
             nc.scalar.activation(
-                factors[:, 1, e : e + 1], bank_b[:, E + e : E + e + 1], FUNC.Copy, scale=factors[:, 0, e : e + 1]
+                factors[:, 1, e : e + 1], factors[:, 1, e : e + 1], FUNC.Copy, scale=factors[:, 0, e : e + 1]
             )
 
         rstd = held.tile([128, E], F32, name="rstd")
@@ -122,26 +122,37 @@ def tile_homelayeroptimized_kernel(
             spread = twice_prob[:, e : e + 1].to_broadcast([128, 128])
             nc.tensor.transpose(gates[e][:], spread, ident[:])
 
-        sums = []
-        for pair in range(E // 2):
-            weighed = []
-            for e in (2 * pair, 2 * pair + 1):
-                active = held.tile([H, N], F32, name=f"active{e}")
-                nc.scalar.activation(
-                    active[:],
-                    products[e],
-                    FUNC.Silu,
-                    bias=affine[:, 1, e : e + 1],
-                    scale=affine[:, 0, e : e + 1],
-                )
-                share = held.tile([H, N], F32, name=f"share{e}")
-                nc.vector.scalar_tensor_tensor(share[:], active[:], 0.5, gates[e][:], ALU.mult, ALU.mult)
-                weighed.append(share)
-            both = held.tile([H, N], F32, name=f"both{pair}")
-            nc.vector.tensor_add(both[:], weighed[0][:], weighed[1][:])
-            sums.append(both)
-        summed = held.tile([H, N], F32, name="summed")
+        active = []
+        for e in range(E):
+            silu = held.tile([H, N], F32, name=f"active{e}")
+            nc.scalar.activation(
+                silu[:],
+                products[e],
+                FUNC.Silu,
+                bias=affine[:, 1, e : e + 1],
+                scale=affine[:, 0, e : e + 1],
+            )
+            active.append(silu)
+        weighed = [held.tile([H, N], F32, name=f"weighed{e}") for e in range(E)]
+        sums = [held.tile([H, N], F32, name=f"sum{pair}") for pair in range(E // 2)]
+        total_sum = held.tile([H, N], F32, name="total_sum")
+
+        def weigh(e, part):
+            nc.vector.scalar_tensor_tensor(
+                weighed[e][:, part], active[e][:, part], 0.5, gates[e][:, part], ALU.mult, ALU.mult
+            )
+
+        def add(pair, part):
+            nc.vector.tensor_add(sums[pair][:, part], weighed[2 * pair][:, part], weighed[2 * pair + 1][:, part])
+
+        everything = slice(0, N)
+        weigh(0, everything)
+        weigh(1, everything)
+        add(0, everything)
+        weigh(2, everything)
         for queue, first in ((nc.sync, 0), (nc.scalar, N // 2)):
             half = slice(first, first + N // 2)
-            nc.vector.tensor_add(summed[:, half], sums[0][:, half], sums[1][:, half])
-            queue.dma_start(out[:, half], summed[:, half])
+            weigh(3, half)
+            add(1, half)
+            nc.vector.tensor_add(total_sum[:, half], sums[0][:, half], sums[1][:, half])
+            queue.dma_start(out[:, half], total_sum[:, half])

@@ -87,7 +87,7 @@ def tile_homelayeroptimized_kernel(
             )
 
         rstd = held.tile([128, E], F32, name="rstd")
-        nc.scalar.activation(rstd[:], var, FUNC.Copy, bias=EPS)
+        nc.vector.tensor_scalar_add(rstd[:], var, EPS)
         nc.gpsimd.tensor_tensor(rstd[:], rstd[:], minus_half[:], ALU.pow)
 
         tanh = held.tile([128, E * E], F32, name="tanh")

@@ -69,13 +69,11 @@ def tile_homelayeroptimized_kernel(
 
         columns_a = E * E + E
         columns_b = 2 * E
-        bank_a = psum.tile([128, columns_a + 2 * N], F32, name="bank_a")
-        bank_b = psum.tile([128, columns_b + 2 * N], F32, name="bank_b")
+        bank_a = psum.tile([128, columns_a + 3 * N], F32, name="bank_a")
+        bank_b = psum.tile([128, columns_b + N], F32, name="bank_b")
         differences, var = bank_a[:, 0 : E * E], bank_a[:, E * E : columns_a]
-        products = []
-        for first in (0, N):
-            products.append(bank_a[:, columns_a + first : columns_a + first + N])
-            products.append(bank_b[:, columns_b + first : columns_b + first + N])
+        products = [bank_a[:, columns_a + e * N : columns_a + (e + 1) * N] for e in range(E - 1)]
+        products.append(bank_b[:, columns_b : columns_b + N])
         nc.tensor.matmul(bank_a[:, 0:columns_a], early[:], differ[:], start=True, stop=True)
         nc.tensor.matmul(bank_b[:, 0:columns_b], later[:], turn[:], start=True, stop=True)
 

@@ -33,9 +33,9 @@ def tile_homelayeroptimized_kernel(
         def as_rows(vector):
             return vector.rearrange("(e i) o -> e (i o)", e=E)
 
+        nc.sync.dma_start(early[E : 2 * E, :], as_rows(run_var))
         nc.sync.dma_start(early[0:E, :], gate_logits)
-        nc.scalar.dma_start(early[E : 2 * E, :], as_rows(run_var))
-        nc.sync.dma_start(later[E : 2 * E, :], as_rows(run_mean))
+        nc.scalar.dma_start(later[E : 2 * E, :], as_rows(run_mean))
         nc.scalar.dma_start(later[2 * E : 3 * E, :], as_rows(bn_w))
         nc.scalar.dma_start(later[0:E, :], as_rows(b))
         nc.sync.dma_start(tokens[:], x)

import concourse.mybir as mybir
from concourse.masks import make_identity

F32 = mybir.dt.float32
BF16 = mybir.dt.bfloat16
U16 = mybir.dt.uint16
ALU = mybir.AluOpType
FUNC = mybir.ActivationFunctionType
AXIS = mybir.AxisListType

D, S, N, E, H = 128, 1024, 128, 4, 128
M = E * H
EPS = 1e-5
FGATE = 0.5
FLOPS = 2 * D * M * N


def tile_homelayeroptimized_kernel(
    tc, x, w, b, bn_w, bn_b, run_mean, run_var, gate_logits, offs, out
):
    nc = tc.nc
    with (
        tc.tile_pool(name="held", bufs=1) as held,
        tc.psum_pool(name="psum", bufs=1) as psum,
    ):
        early = held.tile([2 * E, 128], F32, name="early")
        later = held.tile([3 * E, 128], F32, name="later")
        base = held.tile([H, 2, E], F32, name="base")
        tokens = held.tile([D, S], BF16, name="tokens")
        weights = held.tile([D, M], BF16, name="weights")
        offsets = held.tile([128, N // 16], U16, name="offsets")

        def as_rows(vector):
            return vector.rearrange("(e i) o -> e (i o)", e=E)

        nc.sync.dma_start(early[E : 2 * E, :], as_rows(run_var))
        nc.sync.dma_start(early[0:E, :], gate_logits)
        nc.scalar.dma_start(later[E : 2 * E, :], as_rows(run_mean))
        nc.scalar.dma_start(later[2 * E : 3 * E, :], as_rows(bn_w))
        nc.scalar.dma_start(later[0:E, :], as_rows(b))
        nc.sync.dma_start(tokens[:], x)
        nc.scalar.dma_start(weights[:], w)
        nc.sync.dma_start(offsets[:], offs)
        nc.sync.dma_start(base[:, 1, :], bn_b.rearrange("(e i) o -> i (e o)", e=E))
        nc.vector.memset(base[:, 0, :], 0.0)

        ident = held.tile([128, 128], F32, name="ident")
        nc.vector.memset(ident[:], 0.0)
        make_identity(nc, ident[:], nomemset=True)
        small = ident[0 : 3 * E, 0 : 3 * E]
        minus_half = held.tile([128, E], F32, name="minus_half")
        nc.vector.memset(minus_half[:], -0.5)
        differ = held.tile([2 * E, E * E + E], F32, name="differ")
        unit = small[0 : 2 * E, 0:E]
        nc.vector.tensor_sub(
            differ[:, 0 : E * E].rearrange("k (e t) -> k e t", e=E),
            unit.unsqueeze(2).to_broadcast([2 * E, E, E]),
            unit.unsqueeze(1).to_broadcast([2 * E, E, E]),
        )
        nc.vector.tensor_copy(differ[:, E * E : E * E + E], small[0 : 2 * E, E : 2 * E])
        terms = held.tile([128, E, E + 1], F32, name="terms", tag="terms")
        nc.vector.memset(terms[:], -0.5 * E)
        warm = held.tile([128, E], F32, name="warm")
        nc.scalar.activation(warm[:], minus_half[:], FUNC.Silu)
        turn = held.tile([3 * E, 2 * E], F32, name="turn")
        nc.vector.tensor_scalar_mul(turn[:, 0:E], small[:, 2 * E : 3 * E], FGATE)
        nc.vector.tensor_sub(turn[:, E : 2 * E], small[:, 0:E], small[:, E : 2 * E])
        nc.vector.tensor_scalar_mul(turn[:, E : 2 * E], turn[:, E : 2 * E], 1.0 / FGATE)

        columns_a = E * E + E
        columns_b = 2 * E
        bank_a = psum.tile([128, columns_a + 3 * N], F32, name="bank_a")
        bank_b = psum.tile([128, columns_b + N], F32, name="bank_b")
        differences, var = bank_a[:, 0 : E * E], bank_a[:, E * E : columns_a]
        products = [bank_a[:, columns_a + e * N : columns_a + (e + 1) * N] for e in range(E - 1)]
        products.append(bank_b[:, columns_b : columns_b + N])
        nc.tensor.matmul(bank_a[:, 0:columns_a], early[:], differ[:], start=True, stop=True)
        nc.tensor.matmul(bank_b[:, 0:columns_b], later[:], turn[:], start=True, stop=True)

        factors = held.tile([128, 2, E], F32, name="factors")
        nc.scalar.copy(factors[:], bank_b[:, 0:columns_b].rearrange("p (v e) -> p v e", v=2))
        for e in range(E):
            nc.scalar.activation(
                factors[:, 1, e : e + 1], factors[:, 1, e : e + 1], FUNC.Copy, scale=factors[:, 0, e : e + 1]
            )

        rstd = held.tile([128, E], F32, name="rstd")
        nc.vector.tensor_scalar_add(rstd[:], var, EPS)
        nc.gpsimd.tensor_tensor(rstd[:], rstd[:], minus_half[:], ALU.pow)

        tanh = held.tile([128, E * E], F32, name="tanh")
        nc.scalar.activation(tanh[:], differences, FUNC.Tanh, scale=0.5)
        raised = held.tile([128, E, E], F32, name="raised")
        nc.vector.tensor_scalar(
            raised[:], tanh[:].rearrange("p (e t) -> p e t", e=E), 1.0, 2.0**-24, ALU.add, ALU.max
        )
        nc.vector.reciprocal(terms[:, :, 0:E], raised[:])
        total = held.tile([128, E], F32, name="total")
        nc.vector.tensor_reduce(total[:], terms[:], AXIS.X, ALU.add)
        twice_prob = held.tile([128, E], F32, name="twice_prob")
        nc.vector.reciprocal(twice_prob[:], total[:])

        for e in range(E):
            nc.tensor.matmul(
                products[e],
                weights[:, e * H : (e + 1) * H],
                tokens[:].indirect(offsets[:]),
                start=True,
                stop=True,
            )

        affine = held.tile([128, 2, E], F32, name="affine", tag="terms")
        for e in range(E):
            nc.vector.scalar_tensor_tensor(
                affine[:, :, e], factors[:, :, e], rstd[:, e : e + 1], base[:, :, e], ALU.mult, ALU.add
            )

        gates = [psum.tile([128, N], F32, name=f"gates{e}") for e in range(E)]
        for e in range(E):
            spread = twice_prob[:, e : e + 1].to_broadcast([128, 128])
            nc.tensor.transpose(gates[e][:], spread, ident[:])

        active = []
        for e in range(E):
            silu = held.tile([H, N], F32, name=f"active{e}")
            nc.scalar.activation(
                silu[:],
                products[e],
                FUNC.Silu,
                bias=affine[:, 1, e : e + 1],
                scale=affine[:, 0, e : e + 1],
            )
            active.append(silu)
        weighed = [held.tile([H, N], F32, name=f"weighed{e}") for e in range(E)]
        sums = [held.tile([H, N], F32, name=f"sum{pair}") for pair in range(E // 2)]
        total_sum = held.tile([H, N], F32, name="total_sum")

        def weigh(e, part):
            nc.vector.scalar_tensor_tensor(
                weighed[e][:, part], active[e][:, part], 0.5, gates[e][:, part], ALU.mult, ALU.mult
            )

        def add(pair, part):
            nc.vector.tensor_add(sums[pair][:, part], weighed[2 * pair][:, part], weighed[2 * pair + 1][:, part])

        everything = slice(0, N)
        weigh(0, everything)
        weigh(1, everything)
        add(0, everything)
        weigh(2, everything)
        for queue, first in ((nc.sync, 0), (nc.scalar, N // 2)):
            half = slice(first, first + N // 2)
            weigh(3, half)
            add(1, half)
            nc.vector.tensor_add(total_sum[:, half], sums[0][:, half], sums[1][:, half])
            queue.dma_start(out[:, half], total_sum[:, half])
